import numpy as np
import ml_dtypes


def mxq(x, axis, fmt="e4m3"):
    dtype, down = {"e4m3": (ml_dtypes.float8_e4m3fn, 7), "e5m2": (ml_dtypes.float8_e5m2, 14)}[fmt]
    v = np.moveaxis(np.asarray(x, np.float32).astype(ml_dtypes.bfloat16).astype(np.float64), axis, -1)
    blocks = v.reshape(v.shape[:-1] + (-1, 32))
    amax = np.abs(blocks).max(-1, keepdims=True)
    byte = np.maximum(np.where(amax > 0, np.frexp(amax)[1] - 1 + 127, 0) - down, 1)
    scale = np.exp2(byte - 127.0)
    codes = (blocks / scale).astype(np.float32).astype(dtype).astype(np.float64)
    return np.moveaxis((codes * scale).reshape(v.shape), -1, axis)


WIDE = False


def mx_kscale(k):
    if not WIDE:
        return np.ones(k)
    levels = np.array([10, -10, 5, -5, 0])
    if k % 512:
        return np.exp2(np.random.permutation(np.resize(levels, k // 32))).repeat(32)
    a = np.empty((k // 512, 16))
    for p in range(k // 512):
        a[p, :8] = np.random.permutation(np.resize(levels, 8))
        for g in range(8):
            far = levels[np.abs(levels - a[p, g]) >= 10]
            a[p, g + 8] = far[np.random.randint(len(far))]
    return np.exp2(a.ravel()).repeat(32)


BF16 = ml_dtypes.bfloat16


def bf(x):
    return np.asarray(x, np.float32).astype(BF16)


def f64(x):
    return np.asarray(x).astype(np.float64)


B, D, H, F, K = 8192, 1024, 256, 1024, 128
EPS_LN = 1e-5


def silu(v):
    return v / (1.0 + np.exp(-v))


def setup_inputs():
    s = mx_kscale(D)
    return {"x": bf(np.random.standard_normal((B, D)) * s),
            "W1": bf(np.random.standard_normal((D, H)) / np.sqrt(D) / s[:, None]),
            "b1": bf(0.2 * np.random.standard_normal(H)),
            "g": bf(1.0 + 0.1 * np.random.standard_normal(H)),
            "beta": bf(0.1 * np.random.standard_normal(H))}


def reference(x, W1, b1, g, beta):
    h = silu((mxq(f64(x), 1, "e4m3") @ mxq(f64(W1), 0, "e4m3")) + f64(b1))
    mu = h.mean(-1, keepdims=True)
    var = ((h - mu) ** 2).mean(-1, keepdims=True)
    return (h - mu) / np.sqrt(var + EPS_LN) * f64(g) + f64(beta)

@@ -1,0 +1,248 @@
+from contextlib import ExitStack
+
+import concourse.mybir as mybir
+from concourse.masks import make_identity
+
+F32 = mybir.dt.float32
+BF16 = mybir.dt.bfloat16
+U32 = mybir.dt.uint32
+U8 = mybir.dt.uint8
+FP8X4 = mybir.dt.float8_e4m3fn_x4
+ACT = mybir.ActivationFunctionType
+ALU = mybir.AluOpType
+
+B, D, H = 8192, 1024, 256
+EPS_LN = 1e-5
+FLOPS = 2 * B * D * H
+
+P = 128
+K_PASS = 512
+PASSES = D // K_PASS
+TILES = 4
+GROUP_ROWS = TILES * P
+GROUPS = B // GROUP_ROWS
+WORDS = D // 2
+BLOCKS = WORDS // P
+LOADS_AHEAD = 5
+SCALAR_COPIES = 3
+
+
+def tile_evidentialhead_pa_t_kernel(tc, x, W1, b1, g, beta, out):
+    nc = tc.nc
+    with ExitStack() as stack:
+        const = stack.enter_context(tc.tile_pool(name="const", bufs=1))
+        x_pool = stack.enter_context(tc.tile_pool(name="x", bufs=4))
+        grouped_pool = stack.enter_context(tc.tile_pool(name="grouped", bufs=3))
+        mx_pool = stack.enter_context(tc.tile_pool(name="mx", bufs=2))
+        work = stack.enter_context(tc.tile_pool(name="work", bufs=3))
+        stats = stack.enter_context(tc.tile_pool(name="stats", bufs=4))
+        xt_psum = stack.enter_context(tc.psum_pool(name="xt_psum", bufs=5))
+        z_psum = stack.enter_context(tc.psum_pool(name="z_psum", bufs=3))
+
+        x_tiles, xt_tiles, grouped_tiles, code_tiles, scale_tiles = {}, {}, {}, {}, {}
+        z_tiles, zb_tiles, h_tiles, t_tiles = {}, {}, {}, {}
+        sum_tiles, negmean_tiles, ssq_tiles, rstd_tiles = {}, {}, {}, {}
+
+        def load_x(i, pieces=1):
+            x_sb = x_pool.tile([P, TILES, D], BF16)
+            rows = x[i * GROUP_ROWS : (i + 1) * GROUP_ROWS, :].rearrange("(p n) k -> p n k", n=TILES)
+            count = TILES // pieces
+            for first in range(0, TILES, count):
+                nc.sync.dma_start(
+                    out=x_sb[:, first : first + count, :], in_=rows[:, first : first + count, :]
+                )
+            x_tiles[i] = x_sb
+
+        load_x(0, pieces=TILES)
+
+        w_raw = const.tile([P, PASSES, 4, H], BF16)
+        nc.sync.dma_start(
+            out=w_raw[:].rearrange("p c t h -> p c (t h)"),
+            in_=W1.rearrange("(c p t) h -> p c (t h)", c=PASSES, p=P, t=4),
+        )
+        for i in range(1, LOADS_AHEAD - 3):
+            load_x(i)
+        vec_rows = const.tile([P, 3, H], BF16)
+        nc.vector.memset(vec_rows[:], 0.0)
+        nc.scalar.dma_start(out=vec_rows[0:1, 0, :], in_=b1.rearrange("(o h) -> o h", o=1))
+        nc.scalar.dma_start(out=vec_rows[0:1, 1, :], in_=g.rearrange("(o h) -> o h", o=1))
+        nc.scalar.dma_start(out=vec_rows[0:1, 2, :], in_=beta.rearrange("(o h) -> o h", o=1))
+        ones = const.tile([P, P], BF16)
+        nc.vector.memset(ones[:], 1.0)
+
+        ident = const.tile([P, P], F32)
+        make_identity(nc, ident[:])
+        neg_half = const.tile([P, TILES], F32)
+        nc.vector.memset(neg_half[:], -0.5)
+
+        w_grouped = const.tile([P, PASSES, H, 4], BF16, align_bytes=64)
+        nc.vector.tensor_copy(out=w_grouped[:], in_=w_raw[:].rearrange("p c t h -> p c h t"))
+        w_codes = const.tile([P, PASSES * H], U32, align_bytes=64)
+        w_scales = const.tile([P, PASSES * H], U8, align_bytes=64)
+        nc.vector.quantize_mx(
+            out=w_codes[:].bitcast(FP8X4),
+            scales=w_scales[:],
+            in_=w_grouped[:].rearrange("p c h t -> p (c h t)"),
+        )
+        vec = const.tile([P, 3, H], F32)
+        bias_rows = vec[:, 0:1, :].to_broadcast([P, 2, H])
+        gain = vec[:, 1, :]
+        shift = vec[:, 2, :]
+
+        def spread_vectors():
+            for first in (0, 2):
+                count = min(2, 3 - first)
+                spread = z_psum.tile([P, 2, H], F32, tag="z")
+                nc.tensor.matmul(
+                    out=spread[:, 0:count, :], lhsT=ones[:],
+                    rhs=vec_rows[:, first : first + count, :], start=True, stop=True,
+                )
+                nc.vector.tensor_copy(
+                    out=vec[:, first : first + count, :], in_=spread[:, 0:count, :]
+                )
+
+        def transpose_x(i):
+            x_words = x_tiles[i][:].bitcast(F32)
+            for n in range(TILES):
+                xt = xt_psum.tile([P, BLOCKS, P], F32)
+                for c in range(PASSES):
+                    for u in range(2):
+                        nc.tensor.transpose(
+                            xt[:, 2 * c + u, :],
+                            x_words[:, n, 2 * P * c + u : 2 * P * (c + 1) : 2],
+                            ident[:],
+                        )
+                xt_tiles[(i, n)] = xt
+
+        def copy_xt(i):
+            grouped = grouped_pool.tile([P, PASSES * TILES * P * 4], BF16, align_bytes=64)
+            words = grouped[:].bitcast(F32).rearrange(
+                "p (c n r u) -> p c n r u", c=PASSES, n=TILES, r=P, u=2
+            )
+            for n in range(TILES):
+                planes = xt_tiles[(i, n)][:].rearrange("p (c u) r -> p c r u", c=PASSES, u=2)
+                if n < SCALAR_COPIES:
+                    nc.scalar.copy(out=words[:, :, n, :, :], in_=planes)
+                else:
+                    nc.vector.tensor_copy(out=words[:, :, n, :, :], in_=planes)
+            grouped_tiles[i] = grouped
+
+        def quantise_x(i):
+            codes = mx_pool.tile([P, PASSES * GROUP_ROWS], U32, align_bytes=64)
+            scales = mx_pool.tile([P, PASSES * GROUP_ROWS], U8, align_bytes=64)
+            nc.vector.quantize_mx(
+                out=codes[:].bitcast(FP8X4), scales=scales[:], in_=grouped_tiles[i][:]
+            )
+            code_tiles[i] = codes
+            scale_tiles[i] = scales
+
+        def multiply(i):
+            for half in range(TILES // 2):
+                z = z_psum.tile([P, 2, H], F32, tag="z")
+                for m in range(2):
+                    n = 2 * half + m
+                    for c in range(PASSES):
+                        x_cols = slice(c * GROUP_ROWS + n * P, c * GROUP_ROWS + (n + 1) * P)
+                        w_cols = slice(c * H, (c + 1) * H)
+                        nc.tensor.matmul_mx(
+                            out=z[:, m, :],
+                            lhsT=code_tiles[i][:, x_cols].bitcast(FP8X4),
+                            lhsT_scale=scale_tiles[i][:, x_cols],
+                            rhs=w_codes[:, w_cols].bitcast(FP8X4),
+                            rhs_scale=w_scales[:, w_cols],
+                            start=(c == 0),
+                            stop=(c == PASSES - 1),
+                        )
+                z_tiles[(i, half)] = z
+
+        def add_bias(i):
+            zb = work.tile([P, TILES, H], F32)
+            for half in range(TILES // 2):
+                nc.vector.tensor_tensor(
+                    out=zb[:, 2 * half : 2 * half + 2, :],
+                    in0=z_tiles[(i, half)][:],
+                    in1=bias_rows,
+                    op=ALU.add,
+                )
+            zb_tiles[i] = zb
+
+        def silu(i):
+            h = work.tile([P, TILES, H], F32)
+            h_sum = stats.tile([P, TILES], F32)
+            for n in range(TILES):
+                nc.scalar.activation(
+                    out=h[:, n, :], in_=zb_tiles[i][:, n, :], func=ACT.Silu,
+                    accum_out=h_sum[:, n : n + 1],
+                )
+            h_tiles[i] = h
+            sum_tiles[i] = h_sum
+
+        def variance(i):
+            ssq = stats.tile([P, TILES], F32)
+            for n in range(TILES):
+                squares = work.tile([P, H], F32)
+                nc.scalar.activation(
+                    out=squares[:], in_=h_tiles[i][:, n, :], func=ACT.Square,
+                    scale=-1.0 * H, bias=sum_tiles[i][:, n : n + 1], accum_out=ssq[:, n : n + 1],
+                )
+            ssq_tiles[i] = ssq
+
+        def small_statistics(i):
+            negmean = stats.tile([P, TILES], F32)
+            nc.gpsimd.tensor_scalar(
+                out=negmean[:], in0=sum_tiles[i][:], scalar1=-1.0 / H, scalar2=0.0,
+                op0=ALU.mult, op1=ALU.add,
+            )
+            negmean_tiles[i] = negmean
+            var_eps = stats.tile([P, TILES], F32)
+            nc.gpsimd.tensor_scalar(
+                out=var_eps[:], in0=ssq_tiles[i][:], scalar1=1.0 / (H * H * H), scalar2=EPS_LN,
+                op0=ALU.mult, op1=ALU.add,
+            )
+            rstd = stats.tile([P, TILES], F32)
+            nc.gpsimd.tensor_tensor(out=rstd[:], in0=var_eps[:], in1=neg_half[:], op=ALU.pow)
+            rstd_tiles[i] = rstd
+
+        def centre_and_gain(i):
+            t = work.tile([P, TILES, H], F32)
+            for n in range(TILES):
+                nc.vector.scalar_tensor_tensor(
+                    out=t[:, n, :], in0=h_tiles[i][:, n, :],
+                    scalar=negmean_tiles[i][:, n : n + 1], in1=gain,
+                    op0=ALU.add, op1=ALU.mult,
+                )
+            t_tiles[i] = t
+
+        def scale_shift_store(i):
+            o = work.tile([P, TILES, H], F32)
+            rows = out[i * GROUP_ROWS : (i + 1) * GROUP_ROWS, :].rearrange(
+                "(p n) h -> p n h", n=TILES
+            )
+            for n in range(TILES):
+                nc.vector.scalar_tensor_tensor(
+                    out=o[:, n, :], in0=t_tiles[i][:, n, :],
+                    scalar=rstd_tiles[i][:, n : n + 1], in1=shift,
+                    op0=ALU.mult, op1=ALU.add,
+                )
+                if n % 2 == 1:
+                    nc.sync.dma_start(out=rows[:, n - 1 : n + 1, :], in_=o[:, n - 1 : n + 1, :])
+
+        def run(stage, i):
+            if 0 <= i < GROUPS:
+                stage(i)
+
+        with tc.manual_schedule():
+            for step in range(-3, GROUPS + 2):
+                run(load_x, step + LOADS_AHEAD)
+                run(quantise_x, step + 1)
+                run(copy_xt, step + 2)
+                run(transpose_x, step + 3)
+                if step == -1:
+                    spread_vectors()
+                run(add_bias, step)
+                run(multiply, step + 1)
+                run(silu, step)
+                run(variance, step)
+                run(small_statistics, step)
+                run(centre_and_gain, step - 1)
+                run(scale_shift_store, step - 2)

@@ -24,7 +24,7 @@ GROUPS = B // GROUP_ROWS
 WORDS = D // 2
 BLOCKS = WORDS // P
 LOADS_AHEAD = 5
-SCALAR_COPIES = 3
+SCALAR_COPIES = 4
 
 
 def tile_evidentialhead_pa_t_kernel(tc, x, W1, b1, g, beta, out):

@@ -18,30 +18,30 @@ FLOPS = 2 * B * D * H
 P = 128
 K_PASS = 512
 PASSES = D // K_PASS
+HALVES = H // P
 TILES = 4
+PAIRS = TILES // 2
 GROUP_ROWS = TILES * P
 GROUPS = B // GROUP_ROWS
-WORDS = D // 2
-BLOCKS = WORDS // P
+BLOCKS = D // 2 // P
 LOADS_AHEAD = 5
-SCALAR_COPIES = 4
 
 
 def tile_evidentialhead_pa_t_kernel(tc, x, W1, b1, g, beta, out):
     nc = tc.nc
     with ExitStack() as stack:
         const = stack.enter_context(tc.tile_pool(name="const", bufs=1))
-        x_pool = stack.enter_context(tc.tile_pool(name="x", bufs=4))
+        x_pool = stack.enter_context(tc.tile_pool(name="x", bufs=5))
         grouped_pool = stack.enter_context(tc.tile_pool(name="grouped", bufs=3))
         mx_pool = stack.enter_context(tc.tile_pool(name="mx", bufs=2))
         work = stack.enter_context(tc.tile_pool(name="work", bufs=3))
         stats = stack.enter_context(tc.tile_pool(name="stats", bufs=4))
-        xt_psum = stack.enter_context(tc.psum_pool(name="xt_psum", bufs=5))
-        z_psum = stack.enter_context(tc.psum_pool(name="z_psum", bufs=3))
+        xt_psum = stack.enter_context(tc.psum_pool(name="xt_psum", bufs=4))
+        z_psum = stack.enter_context(tc.psum_pool(name="z_psum", bufs=2))
+        h_psum = stack.enter_context(tc.psum_pool(name="h_psum", bufs=2))
 
         x_tiles, xt_tiles, grouped_tiles, code_tiles, scale_tiles = {}, {}, {}, {}, {}
-        z_tiles, zb_tiles, h_tiles, t_tiles = {}, {}, {}, {}
-        sum_tiles, negmean_tiles, ssq_tiles, rstd_tiles = {}, {}, {}, {}
+        z_tiles, ht_tiles, h_tiles, moment_tiles, rstd_tiles, t_tiles = {}, {}, {}, {}, {}, {}
 
         def load_x(i, pieces=1):
             x_sb = x_pool.tile([P, TILES, D], BF16)
@@ -55,12 +55,13 @@ def tile_evidentialhead_pa_t_kernel(tc, x, W1, b1, g, beta, out):
 
         load_x(0, pieces=TILES)
 
+        load_x(1, pieces=2)
         w_raw = const.tile([P, PASSES, 4, H], BF16)
         nc.sync.dma_start(
             out=w_raw[:].rearrange("p c t h -> p c (t h)"),
             in_=W1.rearrange("(c p t) h -> p c (t h)", c=PASSES, p=P, t=4),
         )
-        for i in range(1, LOADS_AHEAD - 3):
+        for i in range(2, LOADS_AHEAD - 2):
             load_x(i)
         vec_rows = const.tile([P, 3, H], BF16)
         nc.vector.memset(vec_rows[:], 0.0)
@@ -70,6 +71,8 @@ def tile_evidentialhead_pa_t_kernel(tc, x, W1, b1, g, beta, out):
         ones = const.tile([P, P], BF16)
         nc.vector.memset(ones[:], 1.0)
 
+        table = const.tile([P, 1], F32)
+        nc.scalar.activation(out=table[:], in_=ones[:, 0:1], func=ACT.Silu)
         ident = const.tile([P, P], F32)
         make_identity(nc, ident[:])
         neg_half = const.tile([P, TILES], F32)
@@ -84,26 +87,28 @@ def tile_evidentialhead_pa_t_kernel(tc, x, W1, b1, g, beta, out):
             scales=w_scales[:],
             in_=w_grouped[:].rearrange("p c h t -> p (c h t)"),
         )
-        vec = const.tile([P, 3, H], F32)
-        bias_rows = vec[:, 0:1, :].to_broadcast([P, 2, H])
-        gain = vec[:, 1, :]
-        shift = vec[:, 2, :]
+        bias_col = const.tile([P, HALVES], F32)
+        vec = const.tile([P, 2, H], F32)
+        gain = vec[:, 0, :]
+        shift = vec[:, 1, :]
 
         def spread_vectors():
-            for first in (0, 2):
-                count = min(2, 3 - first)
-                spread = z_psum.tile([P, 2, H], F32, tag="z")
+            spread = z_psum.tile([P, 2, H], F32, tag="z")
+            nc.tensor.matmul(
+                out=spread[:], lhsT=ones[:], rhs=vec_rows[:, 1:3, :], start=True, stop=True
+            )
+            nc.vector.tensor_copy(out=vec[:], in_=spread[:])
+            column = z_psum.tile([P, HALVES, 4], F32, tag="z")
+            for half in range(HALVES):
                 nc.tensor.matmul(
-                    out=spread[:, 0:count, :], lhsT=ones[:],
-                    rhs=vec_rows[:, first : first + count, :], start=True, stop=True,
+                    out=column[:, half, :], lhsT=vec_rows[:, 0, half * P : (half + 1) * P],
+                    rhs=ones[:, 0:4], start=True, stop=True,
                 )
-                nc.vector.tensor_copy(
-                    out=vec[:, first : first + count, :], in_=spread[:, 0:count, :]
-                )
+            nc.vector.tensor_copy(out=bias_col[:], in_=column[:, :, 0])
 
-        def transpose_x(i):
+        def transpose_x(i, tiles):
             x_words = x_tiles[i][:].bitcast(F32)
-            for n in range(TILES):
+            for n in tiles:
                 xt = xt_psum.tile([P, BLOCKS, P], F32)
                 for c in range(PASSES):
                     for u in range(2):
@@ -114,18 +119,16 @@ def tile_evidentialhead_pa_t_kernel(tc, x, W1, b1, g, beta, out):
                         )
                 xt_tiles[(i, n)] = xt
 
-        def copy_xt(i):
-            grouped = grouped_pool.tile([P, PASSES * TILES * P * 4], BF16, align_bytes=64)
-            words = grouped[:].bitcast(F32).rearrange(
+        def copy_xt(i, tiles):
+            if i not in grouped_tiles:
+                grouped = grouped_pool.tile([P, PASSES * TILES * P * 4], BF16, align_bytes=64)
+                grouped_tiles[i] = grouped
+            words = grouped_tiles[i][:].bitcast(F32).rearrange(
                 "p (c n r u) -> p c n r u", c=PASSES, n=TILES, r=P, u=2
             )
-            for n in range(TILES):
+            for n in tiles:
                 planes = xt_tiles[(i, n)][:].rearrange("p (c u) r -> p c r u", c=PASSES, u=2)
-                if n < SCALAR_COPIES:
-                    nc.scalar.copy(out=words[:, :, n, :, :], in_=planes)
-                else:
-                    nc.vector.tensor_copy(out=words[:, :, n, :, :], in_=planes)
-            grouped_tiles[i] = grouped
+                nc.scalar.copy(out=words[:, :, n, :, :], in_=planes)
 
         def quantise_x(i):
             codes = mx_pool.tile([P, PASSES * GROUP_ROWS], U32, align_bytes=64)
@@ -137,66 +140,74 @@ def tile_evidentialhead_pa_t_kernel(tc, x, W1, b1, g, beta, out):
             scale_tiles[i] = scales
 
         def multiply(i):
-            for half in range(TILES // 2):
-                z = z_psum.tile([P, 2, H], F32, tag="z")
-                for m in range(2):
-                    n = 2 * half + m
-                    for c in range(PASSES):
-                        x_cols = slice(c * GROUP_ROWS + n * P, c * GROUP_ROWS + (n + 1) * P)
-                        w_cols = slice(c * H, (c + 1) * H)
-                        nc.tensor.matmul_mx(
-                            out=z[:, m, :],
-                            lhsT=code_tiles[i][:, x_cols].bitcast(FP8X4),
-                            lhsT_scale=scale_tiles[i][:, x_cols],
-                            rhs=w_codes[:, w_cols].bitcast(FP8X4),
-                            rhs_scale=w_scales[:, w_cols],
-                            start=(c == 0),
-                            stop=(c == PASSES - 1),
-                        )
+            for half in range(HALVES):
+                z = z_psum.tile([P, GROUP_ROWS], F32, tag="z")
+                for c in range(PASSES):
+                    x_cols = slice(c * GROUP_ROWS, (c + 1) * GROUP_ROWS)
+                    w_cols = slice(c * H + half * P, c * H + (half + 1) * P)
+                    nc.tensor.matmul_mx(
+                        out=z[:],
+                        lhsT=w_codes[:, w_cols].bitcast(FP8X4),
+                        lhsT_scale=w_scales[:, w_cols],
+                        rhs=code_tiles[i][:, x_cols].bitcast(FP8X4),
+                        rhs_scale=scale_tiles[i][:, x_cols],
+                        start=(c == 0),
+                        stop=(c == PASSES - 1),
+                    )
                 z_tiles[(i, half)] = z
 
-        def add_bias(i):
-            zb = work.tile([P, TILES, H], F32)
-            for half in range(TILES // 2):
-                nc.vector.tensor_tensor(
-                    out=zb[:, 2 * half : 2 * half + 2, :],
-                    in0=z_tiles[(i, half)][:],
-                    in1=bias_rows,
-                    op=ALU.add,
-                )
-            zb_tiles[i] = zb
-
         def silu(i):
-            h = work.tile([P, TILES, H], F32)
-            h_sum = stats.tile([P, TILES], F32)
-            for n in range(TILES):
+            ht = work.tile([P, HALVES, GROUP_ROWS], F32)
+            for half in range(HALVES):
                 nc.scalar.activation(
-                    out=h[:, n, :], in_=zb_tiles[i][:, n, :], func=ACT.Silu,
-                    accum_out=h_sum[:, n : n + 1],
+                    out=ht[:, half, :], in_=z_tiles[(i, half)][:], func=ACT.Silu,
+                    bias=bias_col[:, half : half + 1],
                 )
-            h_tiles[i] = h
-            sum_tiles[i] = h_sum
+            ht_tiles[i] = ht
 
-        def variance(i):
-            ssq = stats.tile([P, TILES], F32)
-            for n in range(TILES):
-                squares = work.tile([P, H], F32)
-                nc.scalar.activation(
-                    out=squares[:], in_=h_tiles[i][:, n, :], func=ACT.Square,
-                    scale=-1.0 * H, bias=sum_tiles[i][:, n : n + 1], accum_out=ssq[:, n : n + 1],
-                )
-            ssq_tiles[i] = ssq
+        def transpose_h(i):
+            for pair in range(PAIRS):
+                h = h_psum.tile([P, 2, H], F32)
+                for m in range(2):
+                    n = 2 * pair + m
+                    for half in range(HALVES):
+                        nc.tensor.transpose(
+                            h[:, m, half * P : (half + 1) * P],
+                            ht_tiles[i][:, half, n * P : (n + 1) * P],
+                            ident[:],
+                        )
+                h_tiles[(i, pair)] = h
 
-        def small_statistics(i):
-            negmean = stats.tile([P, TILES], F32)
-            nc.gpsimd.tensor_scalar(
-                out=negmean[:], in0=sum_tiles[i][:], scalar1=-1.0 / H, scalar2=0.0,
-                op0=ALU.mult, op1=ALU.add,
-            )
-            negmean_tiles[i] = negmean
+        def moments(i):
+            moment = stats.tile([P, TILES, 3], F32)
+            for pair in range(PAIRS):
+                h = h_tiles[(i, pair)]
+                if pair == 1 and i % 4 != 3:
+                    for m in range(2):
+                        n = 2 * pair + m
+                        scratch = work.tile([P, H], F32)
+                        nc.scalar.activation(
+                            out=scratch[:], in_=h[:, m, :], func=ACT.Copy, scale=1.0 / H,
+                            accum_out=moment[:, n, 1:2],
+                        )
+                    for m in range(2):
+                        n = 2 * pair + m
+                        scratch = work.tile([P, H], F32)
+                        nc.scalar.activation(
+                            out=scratch[:], in_=h[:, m, :], func=ACT.Square, scale=-1.0,
+                            bias=moment[:, n, 1:2], accum_out=moment[:, n, 2:3],
+                        )
+                else:
+                    nc.vector.bn_stats(
+                        out=moment[:, 2 * pair : 2 * pair + 2, :].rearrange("p m s -> p (m s)"),
+                        in_=h[:].rearrange("p m h -> p h m"),
+                    )
+            moment_tiles[i] = moment
+
+        def rsqrt(i):
             var_eps = stats.tile([P, TILES], F32)
             nc.gpsimd.tensor_scalar(
-                out=var_eps[:], in0=ssq_tiles[i][:], scalar1=1.0 / (H * H * H), scalar2=EPS_LN,
+                out=var_eps[:], in0=moment_tiles[i][:, :, 2], scalar1=1.0 / H, scalar2=EPS_LN,
                 op0=ALU.mult, op1=ALU.add,
             )
             rstd = stats.tile([P, TILES], F32)
@@ -207,9 +218,9 @@ def tile_evidentialhead_pa_t_kernel(tc, x, W1, b1, g, beta, out):
             t = work.tile([P, TILES, H], F32)
             for n in range(TILES):
                 nc.vector.scalar_tensor_tensor(
-                    out=t[:, n, :], in0=h_tiles[i][:, n, :],
-                    scalar=negmean_tiles[i][:, n : n + 1], in1=gain,
-                    op0=ALU.add, op1=ALU.mult,
+                    out=t[:, n, :], in0=h_tiles[(i, n // 2)][:, n % 2, :],
+                    scalar=moment_tiles[i][:, n, 1:2], in1=gain,
+                    op0=ALU.subtract, op1=ALU.mult,
                 )
             t_tiles[i] = t
 
@@ -227,22 +238,25 @@ def tile_evidentialhead_pa_t_kernel(tc, x, W1, b1, g, beta, out):
                 if n % 2 == 1:
                     nc.sync.dma_start(out=rows[:, n - 1 : n + 1, :], in_=o[:, n - 1 : n + 1, :])
 
-        def run(stage, i):
+        def run(stage, i, *args):
             if 0 <= i < GROUPS:
-                stage(i)
+                stage(i, *args)
 
         with tc.manual_schedule():
-            for step in range(-3, GROUPS + 2):
+            for step in range(-2, GROUPS + 2):
                 run(load_x, step + LOADS_AHEAD)
+                run(centre_and_gain, step - 1)
+                run(copy_xt, step + 1, (2,))
+                run(multiply, step)
+                run(silu, step)
+                run(copy_xt, step + 1, (3,))
+                run(scale_shift_store, step - 2)
                 run(quantise_x, step + 1)
-                run(copy_xt, step + 2)
-                run(transpose_x, step + 3)
+                run(transpose_x, step + 2, (0, 1))
+                run(transpose_h, step)
+                run(transpose_x, step + 2, (2, 3))
                 if step == -1:
                     spread_vectors()
-                run(add_bias, step)
-                run(multiply, step + 1)
-                run(silu, step)
-                run(variance, step)
-                run(small_statistics, step)
-                run(centre_and_gain, step - 1)
-                run(scale_shift_store, step - 2)
+                run(copy_xt, step + 2, (0, 1))
+                run(moments, step)
+                run(rsqrt, step)

@@ -19,48 +19,67 @@ P = 128
 K_PASS = 512
 PASSES = D // K_PASS
 HALVES = H // P
-TILES = 4
-PAIRS = TILES // 2
-GROUP_ROWS = TILES * P
-GROUPS = B // GROUP_ROWS
 BLOCKS = D // 2 // P
+SIZES = (4,) * 16
+GROUPS = len(SIZES)
+FIRST = tuple(sum(SIZES[:i]) for i in range(GROUPS))
 LOADS_AHEAD = 5
+XB, XTB, ZBUF, HBUF, WB = 5, 3, 2, 3, 3
+
+
+def STATS_ON_SCALAR(i, pair, n):
+    return n == 1 or (pair == 1 and i % 2 == 0)
+
+
+def EVAC_ON_VECTOR(i, n):
+    return False
 
 
 def tile_evidentialhead_pa_t_kernel(tc, x, W1, b1, g, beta, out):
     nc = tc.nc
     with ExitStack() as stack:
         const = stack.enter_context(tc.tile_pool(name="const", bufs=1))
-        x_pool = stack.enter_context(tc.tile_pool(name="x", bufs=5))
+        x_pool = stack.enter_context(tc.tile_pool(name="x", bufs=XB))
         grouped_pool = stack.enter_context(tc.tile_pool(name="grouped", bufs=3))
         mx_pool = stack.enter_context(tc.tile_pool(name="mx", bufs=2))
-        work = stack.enter_context(tc.tile_pool(name="work", bufs=3))
+        work = stack.enter_context(tc.tile_pool(name="work", bufs=WB))
         stats = stack.enter_context(tc.tile_pool(name="stats", bufs=4))
-        xt_psum = stack.enter_context(tc.psum_pool(name="xt_psum", bufs=4))
-        z_psum = stack.enter_context(tc.psum_pool(name="z_psum", bufs=2))
-        h_psum = stack.enter_context(tc.psum_pool(name="h_psum", bufs=2))
+        xt_psum = stack.enter_context(tc.psum_pool(name="xt_psum", bufs=XTB))
+        z_psum = stack.enter_context(tc.psum_pool(name="z_psum", bufs=ZBUF))
+        h_psum = stack.enter_context(tc.psum_pool(name="h_psum", bufs=HBUF))
 
         x_tiles, xt_tiles, grouped_tiles, code_tiles, scale_tiles = {}, {}, {}, {}, {}
         z_tiles, ht_tiles, h_tiles, moment_tiles, rstd_tiles, t_tiles = {}, {}, {}, {}, {}, {}
+        o_tiles = {}
+
+        def rows_of(dram, i):
+            n = SIZES[i]
+            return dram[FIRST[i] * P : (FIRST[i] + n) * P, :].rearrange("(p n) k -> p n k", n=n)
 
         def load_x(i, pieces=1):
-            x_sb = x_pool.tile([P, TILES, D], BF16)
-            rows = x[i * GROUP_ROWS : (i + 1) * GROUP_ROWS, :].rearrange("(p n) k -> p n k", n=TILES)
-            count = TILES // pieces
-            for first in range(0, TILES, count):
+            n = SIZES[i]
+            x_sb = x_pool.tile([P, n, D], BF16)
+            rows = rows_of(x, i)
+            count = n // pieces
+            for first in range(0, n, count):
                 nc.sync.dma_start(
                     out=x_sb[:, first : first + count, :], in_=rows[:, first : first + count, :]
                 )
             x_tiles[i] = x_sb
 
-        load_x(0, pieces=TILES)
-
-        load_x(1, pieces=2)
+        ones = const.tile([P, P], BF16)
+        nc.vector.memset(ones[:], 1.0)
+        zeros = const.tile([P, 512], BF16)
+        nc.vector.memset(zeros[:], 0.0)
+        ident = const.tile([P, P], F32)
+        make_identity(nc, ident[:])
+        load_x(0, pieces=SIZES[0])
         w_raw = const.tile([P, PASSES, 4, H], BF16)
         nc.sync.dma_start(
             out=w_raw[:].rearrange("p c t h -> p c (t h)"),
             in_=W1.rearrange("(c p t) h -> p c (t h)", c=PASSES, p=P, t=4),
         )
+        load_x(1, pieces=SIZES[1] // 2 if SIZES[1] > 1 else 1)
         for i in range(2, LOADS_AHEAD - 2):
             load_x(i)
         vec_rows = const.tile([P, 3, H], BF16)
@@ -68,36 +87,28 @@ def tile_evidentialhead_pa_t_kernel(tc, x, W1, b1, g, beta, out):
         nc.scalar.dma_start(out=vec_rows[0:1, 0, :], in_=b1.rearrange("(o h) -> o h", o=1))
         nc.scalar.dma_start(out=vec_rows[0:1, 1, :], in_=g.rearrange("(o h) -> o h", o=1))
         nc.scalar.dma_start(out=vec_rows[0:1, 2, :], in_=beta.rearrange("(o h) -> o h", o=1))
-        ones = const.tile([P, P], BF16)
-        nc.vector.memset(ones[:], 1.0)
-
         table = const.tile([P, 1], F32)
         nc.scalar.activation(out=table[:], in_=ones[:, 0:1], func=ACT.Silu)
-        ident = const.tile([P, P], F32)
-        make_identity(nc, ident[:])
-        neg_half = const.tile([P, TILES], F32)
+        neg_half = const.tile([P, 4], F32)
         nc.vector.memset(neg_half[:], -0.5)
-
         w_grouped = const.tile([P, PASSES, H, 4], BF16, align_bytes=64)
-        nc.vector.tensor_copy(out=w_grouped[:], in_=w_raw[:].rearrange("p c t h -> p c h t"))
         w_codes = const.tile([P, PASSES * H], U32, align_bytes=64)
         w_scales = const.tile([P, PASSES * H], U8, align_bytes=64)
-        nc.vector.quantize_mx(
-            out=w_codes[:].bitcast(FP8X4),
-            scales=w_scales[:],
-            in_=w_grouped[:].rearrange("p c h t -> p (c h t)"),
-        )
+
+        def prepare_w():
+            nc.vector.tensor_copy(out=w_grouped[:], in_=w_raw[:].rearrange("p c t h -> p c h t"))
+            nc.vector.quantize_mx(
+                out=w_codes[:].bitcast(FP8X4),
+                scales=w_scales[:],
+                in_=w_grouped[:].rearrange("p c h t -> p (c h t)"),
+            )
+
         bias_col = const.tile([P, HALVES], F32)
         vec = const.tile([P, 2, H], F32)
         gain = vec[:, 0, :]
         shift = vec[:, 1, :]
 
         def spread_vectors():
-            spread = z_psum.tile([P, 2, H], F32, tag="z")
-            nc.tensor.matmul(
-                out=spread[:], lhsT=ones[:], rhs=vec_rows[:, 1:3, :], start=True, stop=True
-            )
-            nc.vector.tensor_copy(out=vec[:], in_=spread[:])
             column = z_psum.tile([P, HALVES, 4], F32, tag="z")
             for half in range(HALVES):
                 nc.tensor.matmul(
@@ -105,10 +116,23 @@ def tile_evidentialhead_pa_t_kernel(tc, x, W1, b1, g, beta, out):
                     rhs=ones[:, 0:4], start=True, stop=True,
                 )
             nc.vector.tensor_copy(out=bias_col[:], in_=column[:, :, 0])
+            spread = z_psum.tile([P, 2, H], F32, tag="z")
+            nc.tensor.matmul(
+                out=spread[:], lhsT=ones[:], rhs=vec_rows[:, 1:3, :], start=True, stop=True
+            )
+            nc.vector.tensor_copy(out=vec[:], in_=spread[:])
 
-        def transpose_x(i, tiles):
+        def warm(count, cols=512):
+            for k in range(count):
+                idle = h_psum.tile([P, 512], F32, tag="h")
+                nc.tensor.matmul(
+                    out=idle[:, 0:cols], lhsT=ones[:], rhs=zeros[:, 0:cols], start=True, stop=True
+                )
+
+        def transpose_x(i, part=0, parts=1):
             x_words = x_tiles[i][:].bitcast(F32)
-            for n in tiles:
+            s = SIZES[i]
+            for n in range(part * s // parts, (part + 1) * s // parts):
                 xt = xt_psum.tile([P, BLOCKS, P], F32)
                 for c in range(PASSES):
                     for u in range(2):
@@ -119,31 +143,37 @@ def tile_evidentialhead_pa_t_kernel(tc, x, W1, b1, g, beta, out):
                         )
                 xt_tiles[(i, n)] = xt
 
-        def copy_xt(i, tiles):
+        def copy_xt(i, part=0, parts=1):
+            s = SIZES[i]
             if i not in grouped_tiles:
-                grouped = grouped_pool.tile([P, PASSES * TILES * P * 4], BF16, align_bytes=64)
+                grouped = grouped_pool.tile([P, PASSES * s * P * 4], BF16, align_bytes=64)
                 grouped_tiles[i] = grouped
             words = grouped_tiles[i][:].bitcast(F32).rearrange(
-                "p (c n r u) -> p c n r u", c=PASSES, n=TILES, r=P, u=2
+                "p (c n r u) -> p c n r u", c=PASSES, n=s, r=P, u=2
             )
-            for n in tiles:
+            for n in range(part * s // parts, (part + 1) * s // parts):
                 planes = xt_tiles[(i, n)][:].rearrange("p (c u) r -> p c r u", c=PASSES, u=2)
-                nc.scalar.copy(out=words[:, :, n, :, :], in_=planes)
+                if EVAC_ON_VECTOR(i, n):
+                    nc.vector.tensor_copy(out=words[:, :, n, :, :], in_=planes)
+                else:
+                    nc.scalar.copy(out=words[:, :, n, :, :], in_=planes)
 
         def quantise_x(i):
-            codes = mx_pool.tile([P, PASSES * GROUP_ROWS], U32, align_bytes=64)
-            scales = mx_pool.tile([P, PASSES * GROUP_ROWS], U8, align_bytes=64)
+            cols = SIZES[i] * P
+            codes = mx_pool.tile([P, PASSES * cols], U32, align_bytes=64)
+            scales = mx_pool.tile([P, PASSES * cols], U8, align_bytes=64)
             nc.vector.quantize_mx(
                 out=codes[:].bitcast(FP8X4), scales=scales[:], in_=grouped_tiles[i][:]
             )
             code_tiles[i] = codes
             scale_tiles[i] = scales
 
-        def multiply(i):
-            for half in range(HALVES):
-                z = z_psum.tile([P, GROUP_ROWS], F32, tag="z")
+        def multiply(i, halves=(0, 1)):
+            cols = SIZES[i] * P
+            for half in halves:
+                z = z_psum.tile([P, cols], F32, tag="z")
                 for c in range(PASSES):
-                    x_cols = slice(c * GROUP_ROWS, (c + 1) * GROUP_ROWS)
+                    x_cols = slice(c * cols, (c + 1) * cols)
                     w_cols = slice(c * H + half * P, c * H + (half + 1) * P)
                     nc.tensor.matmul_mx(
                         out=z[:],
@@ -156,19 +186,26 @@ def tile_evidentialhead_pa_t_kernel(tc, x, W1, b1, g, beta, out):
                     )
                 z_tiles[(i, half)] = z
 
-        def silu(i):
-            ht = work.tile([P, HALVES, GROUP_ROWS], F32)
-            for half in range(HALVES):
+        def silu(i, halves=(0, 1)):
+            if i not in ht_tiles:
+                ht = work.tile([P, HALVES, SIZES[i] * P], F32)
+                ht_tiles[i] = ht
+            for half in halves:
                 nc.scalar.activation(
-                    out=ht[:, half, :], in_=z_tiles[(i, half)][:], func=ACT.Silu,
+                    out=ht_tiles[i][:, half, :], in_=z_tiles[(i, half)][:], func=ACT.Silu,
                     bias=bias_col[:, half : half + 1],
                 )
-            ht_tiles[i] = ht
 
-        def transpose_h(i):
-            for pair in range(PAIRS):
-                h = h_psum.tile([P, 2, H], F32)
-                for m in range(2):
+        def pairs_of(i):
+            return range((SIZES[i] + 1) // 2)
+
+        def transpose_h(i, pairs=None):
+            for pair in (pairs_of(i) if pairs is None else pairs):
+                if pair not in pairs_of(i):
+                    continue
+                width = min(2, SIZES[i])
+                h = h_psum.tile([P, width, H], F32, tag="h")
+                for m in range(width):
                     n = 2 * pair + m
                     for half in range(HALVES):
                         nc.tensor.transpose(
@@ -178,19 +215,25 @@ def tile_evidentialhead_pa_t_kernel(tc, x, W1, b1, g, beta, out):
                         )
                 h_tiles[(i, pair)] = h
 
-        def moments(i):
-            moment = stats.tile([P, TILES, 3], F32)
-            for pair in range(PAIRS):
+        def moments(i, pairs=None):
+            if i not in moment_tiles:
+                moment = stats.tile([P, SIZES[i], 3], F32)
+                moment_tiles[i] = moment
+            moment = moment_tiles[i]
+            width = min(2, SIZES[i])
+            for pair in (pairs_of(i) if pairs is None else pairs):
+                if pair not in pairs_of(i):
+                    continue
                 h = h_tiles[(i, pair)]
-                if pair == 1 and i % 4 != 3:
-                    for m in range(2):
+                if STATS_ON_SCALAR(i, pair, SIZES[i]):
+                    for m in range(width):
                         n = 2 * pair + m
                         scratch = work.tile([P, H], F32)
                         nc.scalar.activation(
                             out=scratch[:], in_=h[:, m, :], func=ACT.Copy, scale=1.0 / H,
                             accum_out=moment[:, n, 1:2],
                         )
-                    for m in range(2):
+                    for m in range(width):
                         n = 2 * pair + m
                         scratch = work.tile([P, H], F32)
                         nc.scalar.activation(
@@ -202,61 +245,68 @@ def tile_evidentialhead_pa_t_kernel(tc, x, W1, b1, g, beta, out):
                         out=moment[:, 2 * pair : 2 * pair + 2, :].rearrange("p m s -> p (m s)"),
                         in_=h[:].rearrange("p m h -> p h m"),
                     )
-            moment_tiles[i] = moment
 
         def rsqrt(i):
-            var_eps = stats.tile([P, TILES], F32)
+            n = SIZES[i]
+            var_eps = stats.tile([P, n], F32)
             nc.gpsimd.tensor_scalar(
                 out=var_eps[:], in0=moment_tiles[i][:, :, 2], scalar1=1.0 / H, scalar2=EPS_LN,
                 op0=ALU.mult, op1=ALU.add,
             )
-            rstd = stats.tile([P, TILES], F32)
-            nc.gpsimd.tensor_tensor(out=rstd[:], in0=var_eps[:], in1=neg_half[:], op=ALU.pow)
+            rstd = stats.tile([P, n], F32)
+            nc.gpsimd.tensor_tensor(out=rstd[:], in0=var_eps[:], in1=neg_half[:, 0:n], op=ALU.pow)
             rstd_tiles[i] = rstd
 
-        def centre_and_gain(i):
-            t = work.tile([P, TILES, H], F32)
-            for n in range(TILES):
-                nc.vector.scalar_tensor_tensor(
-                    out=t[:, n, :], in0=h_tiles[(i, n // 2)][:, n % 2, :],
-                    scalar=moment_tiles[i][:, n, 1:2], in1=gain,
-                    op0=ALU.subtract, op1=ALU.mult,
-                )
-            t_tiles[i] = t
+        def centre_and_gain(i, pairs=None):
+            if i not in t_tiles:
+                t = work.tile([P, SIZES[i], H], F32)
+                t_tiles[i] = t
+            for pair in (pairs_of(i) if pairs is None else pairs):
+                for n in range(2 * pair, min(2 * pair + 2, SIZES[i])):
+                    nc.vector.scalar_tensor_tensor(
+                        out=t_tiles[i][:, n, :], in0=h_tiles[(i, n // 2)][:, n % 2, :],
+                        scalar=moment_tiles[i][:, n, 1:2], in1=gain,
+                        op0=ALU.subtract, op1=ALU.mult,
+                    )
 
         def scale_shift_store(i):
-            o = work.tile([P, TILES, H], F32)
-            rows = out[i * GROUP_ROWS : (i + 1) * GROUP_ROWS, :].rearrange(
-                "(p n) h -> p n h", n=TILES
-            )
-            for n in range(TILES):
+            s = SIZES[i]
+            o = work.tile([P, s, H], F32)
+            rows = rows_of(out, i)
+            for n in range(s):
                 nc.vector.scalar_tensor_tensor(
                     out=o[:, n, :], in0=t_tiles[i][:, n, :],
                     scalar=rstd_tiles[i][:, n : n + 1], in1=shift,
                     op0=ALU.mult, op1=ALU.add,
                 )
-                if n % 2 == 1:
-                    nc.sync.dma_start(out=rows[:, n - 1 : n + 1, :], in_=o[:, n - 1 : n + 1, :])
+                if n % 2 == 1 or s == 1:
+                    first = max(0, n - 1)
+                    nc.sync.dma_start(out=rows[:, first : n + 1, :], in_=o[:, first : n + 1, :])
 
         def run(stage, i, *args):
             if 0 <= i < GROUPS:
                 stage(i, *args)
 
         with tc.manual_schedule():
+            warm(4)
+            prepare_w()
             for step in range(-2, GROUPS + 2):
                 run(load_x, step + LOADS_AHEAD)
-                run(centre_and_gain, step - 1)
-                run(copy_xt, step + 1, (2,))
-                run(multiply, step)
-                run(silu, step)
-                run(copy_xt, step + 1, (3,))
-                run(scale_shift_store, step - 2)
+                run(moments, step - 1)
+                run(multiply, step, (0,))
+                run(silu, step, (0,))
                 run(quantise_x, step + 1)
-                run(transpose_x, step + 2, (0, 1))
-                run(transpose_h, step)
-                run(transpose_x, step + 2, (2, 3))
+                run(transpose_x, step + 2, 0, 2)
+                run(copy_xt, step + 2, 0, 4)
                 if step == -1:
                     spread_vectors()
-                run(copy_xt, step + 2, (0, 1))
-                run(moments, step)
-                run(rsqrt, step)
+                run(multiply, step, (1,))
+                run(silu, step, (1,))
+                run(centre_and_gain, step - 1)
+                run(rsqrt, step - 1)
+                run(transpose_x, step + 2, 1, 2)
+                run(copy_xt, step + 2, 1, 4)
+                run(copy_xt, step + 2, 2, 4)
+                run(copy_xt, step + 2, 3, 4)
+                run(transpose_h, step)
+                run(scale_shift_store, step - 2)

@@ -288,7 +288,7 @@ def tile_evidentialhead_pa_t_kernel(tc, x, W1, b1, g, beta, out):
                 stage(i, *args)
 
         with tc.manual_schedule():
-            warm(4)
+            warm(3)
             prepare_w()
             for step in range(-2, GROUPS + 2):
                 run(load_x, step + LOADS_AHEAD)
@@ -305,6 +305,8 @@ def tile_evidentialhead_pa_t_kernel(tc, x, W1, b1, g, beta, out):
                 run(centre_and_gain, step - 1)
                 run(rsqrt, step - 1)
                 run(transpose_x, step + 2, 1, 2)
+                if step == -2:
+                    warm(3)
                 run(copy_xt, step + 2, 1, 4)
                 run(copy_xt, step + 2, 2, 4)
                 run(copy_xt, step + 2, 3, 4)

@@ -16,87 +16,87 @@ EPS_LN = 1e-5
 FLOPS = 2 * B * D * H
 
 P = 128
-K_PASS = 512
-PASSES = D // K_PASS
+PASSES = D // (4 * P)
 HALVES = H // P
 BLOCKS = D // 2 // P
-SIZES = (4,) * 16
-GROUPS = len(SIZES)
-FIRST = tuple(sum(SIZES[:i]) for i in range(GROUPS))
+PAIR_ROWS = 2 * P
+PAIRS = B // PAIR_ROWS
+LOAD_PAIRS = 2
+TILES = 2 * LOAD_PAIRS
+LOADS = PAIRS // LOAD_PAIRS
 LOADS_AHEAD = 5
-XB, XTB, ZBUF, HBUF, WB = 5, 3, 2, 3, 3
+WARM_COLS = 512
 
 
-def STATS_ON_SCALAR(i, pair, n):
-    return n == 1 or (pair == 1 and i % 2 == 0)
-
-
-def EVAC_ON_VECTOR(i, n):
-    return False
+def on_scalar(j):
+    return j % 3 == 1
 
 
 def tile_evidentialhead_pa_t_kernel(tc, x, W1, b1, g, beta, out):
     nc = tc.nc
     with ExitStack() as stack:
         const = stack.enter_context(tc.tile_pool(name="const", bufs=1))
-        x_pool = stack.enter_context(tc.tile_pool(name="x", bufs=XB))
-        grouped_pool = stack.enter_context(tc.tile_pool(name="grouped", bufs=3))
-        mx_pool = stack.enter_context(tc.tile_pool(name="mx", bufs=2))
-        work = stack.enter_context(tc.tile_pool(name="work", bufs=WB))
-        stats = stack.enter_context(tc.tile_pool(name="stats", bufs=4))
-        xt_psum = stack.enter_context(tc.psum_pool(name="xt_psum", bufs=XTB))
-        z_psum = stack.enter_context(tc.psum_pool(name="z_psum", bufs=ZBUF))
-        h_psum = stack.enter_context(tc.psum_pool(name="h_psum", bufs=HBUF))
+        x_pool = stack.enter_context(tc.tile_pool(name="x", bufs=6))
+        grouped_pool = stack.enter_context(tc.tile_pool(name="grouped", bufs=5))
+        mx_pool = stack.enter_context(tc.tile_pool(name="mx", bufs=4))
+        work = stack.enter_context(tc.tile_pool(name="work", bufs=7))
+        stats = stack.enter_context(tc.tile_pool(name="stats", bufs=5))
+        xt_psum = stack.enter_context(tc.psum_pool(name="xt_psum", bufs=3))
+        z_psum = stack.enter_context(tc.psum_pool(name="z_psum", bufs=2))
+        h_psum = stack.enter_context(tc.psum_pool(name="h_psum", bufs=3))
 
         x_tiles, xt_tiles, grouped_tiles, code_tiles, scale_tiles = {}, {}, {}, {}, {}
         z_tiles, ht_tiles, h_tiles, moment_tiles, rstd_tiles, t_tiles = {}, {}, {}, {}, {}, {}
-        o_tiles = {}
 
         def rows_of(dram, i):
-            n = SIZES[i]
-            return dram[FIRST[i] * P : (FIRST[i] + n) * P, :].rearrange("(p n) k -> p n k", n=n)
+            rows = dram[i * TILES * P : (i + 1) * TILES * P, :]
+            return rows.rearrange("(p n) k -> p n k", n=TILES)
+
+        def tile_of(j, m):
+            return j // LOAD_PAIRS, 2 * (j % LOAD_PAIRS) + m
 
         def load_x(i, pieces=1):
-            n = SIZES[i]
-            x_sb = x_pool.tile([P, n, D], BF16)
-            rows = rows_of(x, i)
-            count = n // pieces
-            for first in range(0, n, count):
-                nc.sync.dma_start(
-                    out=x_sb[:, first : first + count, :], in_=rows[:, first : first + count, :]
-                )
+            x_sb = x_pool.tile([P, TILES, D], BF16)
+            count = TILES // pieces
+            for n in range(0, TILES, count):
+                nc.sync.dma_start(out=x_sb[:, n : n + count, :], in_=rows_of(x, i)[:, n : n + count, :])
             x_tiles[i] = x_sb
 
         ones = const.tile([P, P], BF16)
         nc.vector.memset(ones[:], 1.0)
-        zeros = const.tile([P, 512], BF16)
+        zeros = const.tile([P, WARM_COLS], BF16)
         nc.vector.memset(zeros[:], 0.0)
+        table = const.tile([P, 1], F32)
+        nc.scalar.activation(out=table[:], in_=ones[:, 0:1], func=ACT.Silu)
         ident = const.tile([P, P], F32)
         make_identity(nc, ident[:])
-        load_x(0, pieces=SIZES[0])
+
+        load_x(0, pieces=4)
         w_raw = const.tile([P, PASSES, 4, H], BF16)
         nc.sync.dma_start(
             out=w_raw[:].rearrange("p c t h -> p c (t h)"),
             in_=W1.rearrange("(c p t) h -> p c (t h)", c=PASSES, p=P, t=4),
         )
-        load_x(1, pieces=SIZES[1] // 2 if SIZES[1] > 1 else 1)
-        for i in range(2, LOADS_AHEAD - 2):
-            load_x(i)
+        load_x(1, pieces=2)
+        load_x(2)
         vec_rows = const.tile([P, 3, H], BF16)
         nc.vector.memset(vec_rows[:], 0.0)
         nc.scalar.dma_start(out=vec_rows[0:1, 0, :], in_=b1.rearrange("(o h) -> o h", o=1))
         nc.scalar.dma_start(out=vec_rows[0:1, 1, :], in_=g.rearrange("(o h) -> o h", o=1))
         nc.scalar.dma_start(out=vec_rows[0:1, 2, :], in_=beta.rearrange("(o h) -> o h", o=1))
-        table = const.tile([P, 1], F32)
-        nc.scalar.activation(out=table[:], in_=ones[:, 0:1], func=ACT.Silu)
-        neg_half = const.tile([P, 4], F32)
+        for i in range(3, LOADS_AHEAD):
+            load_x(i)
+        neg_half = const.tile([P, TILES], F32)
         nc.vector.memset(neg_half[:], -0.5)
+
         w_grouped = const.tile([P, PASSES, H, 4], BF16, align_bytes=64)
         w_codes = const.tile([P, PASSES * H], U32, align_bytes=64)
         w_scales = const.tile([P, PASSES * H], U8, align_bytes=64)
 
-        def prepare_w():
+        def group_w():
             nc.vector.tensor_copy(out=w_grouped[:], in_=w_raw[:].rearrange("p c t h -> p c h t"))
+
+        def quantise_w():
             nc.vector.quantize_mx(
                 out=w_codes[:].bitcast(FP8X4),
                 scales=w_scales[:],
@@ -109,206 +109,185 @@ def tile_evidentialhead_pa_t_kernel(tc, x, W1, b1, g, beta, out):
         shift = vec[:, 1, :]
 
         def spread_vectors():
-            column = z_psum.tile([P, HALVES, 4], F32, tag="z")
+            column = h_psum.tile([P, HALVES, 4], F32, tag="h")
             for half in range(HALVES):
                 nc.tensor.matmul(
                     out=column[:, half, :], lhsT=vec_rows[:, 0, half * P : (half + 1) * P],
                     rhs=ones[:, 0:4], start=True, stop=True,
                 )
-            nc.vector.tensor_copy(out=bias_col[:], in_=column[:, :, 0])
-            spread = z_psum.tile([P, 2, H], F32, tag="z")
+            spread = h_psum.tile([P, 2, H], F32, tag="h")
             nc.tensor.matmul(
                 out=spread[:], lhsT=ones[:], rhs=vec_rows[:, 1:3, :], start=True, stop=True
             )
-            nc.vector.tensor_copy(out=vec[:], in_=spread[:])
+            return column, spread
 
-        def warm(count, cols=512):
+        def warm(count):
             for k in range(count):
-                idle = h_psum.tile([P, 512], F32, tag="h")
-                nc.tensor.matmul(
-                    out=idle[:, 0:cols], lhsT=ones[:], rhs=zeros[:, 0:cols], start=True, stop=True
-                )
+                idle = h_psum.tile([P, WARM_COLS], F32, tag="h")
+                nc.tensor.matmul(out=idle[:], lhsT=ones[:], rhs=zeros[:], start=True, stop=True)
 
-        def transpose_x(i, part=0, parts=1):
+        def transpose_x(j, m):
+            i, n = tile_of(j, m)
             x_words = x_tiles[i][:].bitcast(F32)
-            s = SIZES[i]
-            for n in range(part * s // parts, (part + 1) * s // parts):
-                xt = xt_psum.tile([P, BLOCKS, P], F32)
-                for c in range(PASSES):
-                    for u in range(2):
-                        nc.tensor.transpose(
-                            xt[:, 2 * c + u, :],
-                            x_words[:, n, 2 * P * c + u : 2 * P * (c + 1) : 2],
-                            ident[:],
-                        )
-                xt_tiles[(i, n)] = xt
+            xt = xt_psum.tile([P, BLOCKS, P], F32)
+            for c in range(PASSES):
+                for u in range(2):
+                    nc.tensor.transpose(
+                        xt[:, 2 * c + u, :],
+                        x_words[:, n, 2 * P * c + u : 2 * P * (c + 1) : 2],
+                        ident[:],
+                    )
+            xt_tiles[(j, m)] = xt
 
-        def copy_xt(i, part=0, parts=1):
-            s = SIZES[i]
-            if i not in grouped_tiles:
-                grouped = grouped_pool.tile([P, PASSES * s * P * 4], BF16, align_bytes=64)
-                grouped_tiles[i] = grouped
-            words = grouped_tiles[i][:].bitcast(F32).rearrange(
-                "p (c n r u) -> p c n r u", c=PASSES, n=s, r=P, u=2
+        def copy_xt(j, m):
+            if j not in grouped_tiles:
+                grouped = grouped_pool.tile([P, PASSES * PAIR_ROWS * 4], BF16, align_bytes=64)
+                grouped_tiles[j] = grouped
+            words = grouped_tiles[j][:].bitcast(F32).rearrange(
+                "p (c m r u) -> p c m r u", c=PASSES, m=2, r=P, u=2
             )
-            for n in range(part * s // parts, (part + 1) * s // parts):
-                planes = xt_tiles[(i, n)][:].rearrange("p (c u) r -> p c r u", c=PASSES, u=2)
-                if EVAC_ON_VECTOR(i, n):
-                    nc.vector.tensor_copy(out=words[:, :, n, :, :], in_=planes)
-                else:
-                    nc.scalar.copy(out=words[:, :, n, :, :], in_=planes)
+            planes = xt_tiles[(j, m)][:].rearrange("p (c u) r -> p c r u", c=PASSES, u=2)
+            nc.scalar.copy(out=words[:, :, m, :, :], in_=planes)
 
-        def quantise_x(i):
-            cols = SIZES[i] * P
-            codes = mx_pool.tile([P, PASSES * cols], U32, align_bytes=64)
-            scales = mx_pool.tile([P, PASSES * cols], U8, align_bytes=64)
+        def quantise_x(j):
+            codes = mx_pool.tile([P, PASSES * PAIR_ROWS], U32, align_bytes=64)
+            scales = mx_pool.tile([P, PASSES * PAIR_ROWS], U8, align_bytes=64)
             nc.vector.quantize_mx(
-                out=codes[:].bitcast(FP8X4), scales=scales[:], in_=grouped_tiles[i][:]
+                out=codes[:].bitcast(FP8X4), scales=scales[:], in_=grouped_tiles[j][:]
             )
-            code_tiles[i] = codes
-            scale_tiles[i] = scales
+            code_tiles[j] = codes
+            scale_tiles[j] = scales
 
-        def multiply(i, halves=(0, 1)):
-            cols = SIZES[i] * P
-            for half in halves:
-                z = z_psum.tile([P, cols], F32, tag="z")
+        def multiply(j):
+            z = z_psum.tile([P, HALVES, PAIR_ROWS], F32)
+            for half in range(HALVES):
                 for c in range(PASSES):
-                    x_cols = slice(c * cols, (c + 1) * cols)
+                    x_cols = slice(c * PAIR_ROWS, (c + 1) * PAIR_ROWS)
                     w_cols = slice(c * H + half * P, c * H + (half + 1) * P)
                     nc.tensor.matmul_mx(
-                        out=z[:],
+                        out=z[:, half, :],
                         lhsT=w_codes[:, w_cols].bitcast(FP8X4),
                         lhsT_scale=w_scales[:, w_cols],
-                        rhs=code_tiles[i][:, x_cols].bitcast(FP8X4),
-                        rhs_scale=scale_tiles[i][:, x_cols],
+                        rhs=code_tiles[j][:, x_cols].bitcast(FP8X4),
+                        rhs_scale=scale_tiles[j][:, x_cols],
                         start=(c == 0),
                         stop=(c == PASSES - 1),
                     )
-                z_tiles[(i, half)] = z
+            z_tiles[j] = z
 
-        def silu(i, halves=(0, 1)):
-            if i not in ht_tiles:
-                ht = work.tile([P, HALVES, SIZES[i] * P], F32)
-                ht_tiles[i] = ht
-            for half in halves:
+        def silu(j):
+            ht = work.tile([P, HALVES, PAIR_ROWS], F32)
+            for half in range(HALVES):
                 nc.scalar.activation(
-                    out=ht_tiles[i][:, half, :], in_=z_tiles[(i, half)][:], func=ACT.Silu,
+                    out=ht[:, half, :], in_=z_tiles[j][:, half, :], func=ACT.Silu,
                     bias=bias_col[:, half : half + 1],
                 )
+            ht_tiles[j] = ht
 
-        def pairs_of(i):
-            return range((SIZES[i] + 1) // 2)
-
-        def transpose_h(i, pairs=None):
-            for pair in (pairs_of(i) if pairs is None else pairs):
-                if pair not in pairs_of(i):
-                    continue
-                width = min(2, SIZES[i])
-                h = h_psum.tile([P, width, H], F32, tag="h")
-                for m in range(width):
-                    n = 2 * pair + m
-                    for half in range(HALVES):
-                        nc.tensor.transpose(
-                            h[:, m, half * P : (half + 1) * P],
-                            ht_tiles[i][:, half, n * P : (n + 1) * P],
-                            ident[:],
-                        )
-                h_tiles[(i, pair)] = h
-
-        def moments(i, pairs=None):
-            if i not in moment_tiles:
-                moment = stats.tile([P, SIZES[i], 3], F32)
-                moment_tiles[i] = moment
-            moment = moment_tiles[i]
-            width = min(2, SIZES[i])
-            for pair in (pairs_of(i) if pairs is None else pairs):
-                if pair not in pairs_of(i):
-                    continue
-                h = h_tiles[(i, pair)]
-                if STATS_ON_SCALAR(i, pair, SIZES[i]):
-                    for m in range(width):
-                        n = 2 * pair + m
-                        scratch = work.tile([P, H], F32)
-                        nc.scalar.activation(
-                            out=scratch[:], in_=h[:, m, :], func=ACT.Copy, scale=1.0 / H,
-                            accum_out=moment[:, n, 1:2],
-                        )
-                    for m in range(width):
-                        n = 2 * pair + m
-                        scratch = work.tile([P, H], F32)
-                        nc.scalar.activation(
-                            out=scratch[:], in_=h[:, m, :], func=ACT.Square, scale=-1.0,
-                            bias=moment[:, n, 1:2], accum_out=moment[:, n, 2:3],
-                        )
-                else:
-                    nc.vector.bn_stats(
-                        out=moment[:, 2 * pair : 2 * pair + 2, :].rearrange("p m s -> p (m s)"),
-                        in_=h[:].rearrange("p m h -> p h m"),
+        def transpose_h(j):
+            h = h_psum.tile([P, 2, H], F32, tag="h")
+            for m in range(2):
+                for half in range(HALVES):
+                    nc.tensor.transpose(
+                        h[:, m, half * P : (half + 1) * P],
+                        ht_tiles[j][:, half, m * P : (m + 1) * P],
+                        ident[:],
                     )
+            h_tiles[j] = h
 
-        def rsqrt(i):
-            n = SIZES[i]
-            var_eps = stats.tile([P, n], F32)
+        def moments(j):
+            i, first = tile_of(j, 0)
+            if first == 0:
+                moment_load = stats.tile([P, TILES, 3], F32)
+                moment_tiles[i] = moment_load
+            moment = moment_tiles[i][:, first : first + 2, :]
+            h = h_tiles[j]
+            if on_scalar(j):
+                for m in range(2):
+                    scratch = work.tile([P, H], F32)
+                    nc.scalar.activation(
+                        out=scratch[:], in_=h[:, m, :], func=ACT.Copy, scale=1.0 / H,
+                        accum_out=moment[:, m, 1:2],
+                    )
+                for m in range(2):
+                    scratch = work.tile([P, H], F32)
+                    nc.scalar.activation(
+                        out=scratch[:], in_=h[:, m, :], func=ACT.Square, scale=-1.0,
+                        bias=moment[:, m, 1:2], accum_out=moment[:, m, 2:3],
+                    )
+            else:
+                nc.vector.bn_stats(
+                    out=moment.rearrange("p m s -> p (m s)"), in_=h[:].rearrange("p m h -> p h m")
+                )
+
+        def rsqrt(j):
+            i, first = tile_of(j, 0)
+            if first == 0:
+                return
+            var_eps = stats.tile([P, TILES], F32)
             nc.gpsimd.tensor_scalar(
                 out=var_eps[:], in0=moment_tiles[i][:, :, 2], scalar1=1.0 / H, scalar2=EPS_LN,
                 op0=ALU.mult, op1=ALU.add,
             )
-            rstd = stats.tile([P, n], F32)
-            nc.gpsimd.tensor_tensor(out=rstd[:], in0=var_eps[:], in1=neg_half[:, 0:n], op=ALU.pow)
+            rstd = stats.tile([P, TILES], F32)
+            nc.gpsimd.tensor_tensor(out=rstd[:], in0=var_eps[:], in1=neg_half[:], op=ALU.pow)
             rstd_tiles[i] = rstd
 
-        def centre_and_gain(i, pairs=None):
-            if i not in t_tiles:
-                t = work.tile([P, SIZES[i], H], F32)
-                t_tiles[i] = t
-            for pair in (pairs_of(i) if pairs is None else pairs):
-                for n in range(2 * pair, min(2 * pair + 2, SIZES[i])):
-                    nc.vector.scalar_tensor_tensor(
-                        out=t_tiles[i][:, n, :], in0=h_tiles[(i, n // 2)][:, n % 2, :],
-                        scalar=moment_tiles[i][:, n, 1:2], in1=gain,
-                        op0=ALU.subtract, op1=ALU.mult,
-                    )
-
-        def scale_shift_store(i):
-            s = SIZES[i]
-            o = work.tile([P, s, H], F32)
-            rows = rows_of(out, i)
-            for n in range(s):
+        def centre_and_gain(j):
+            i, first = tile_of(j, 0)
+            t = work.tile([P, 2, H], F32)
+            for m in range(2):
                 nc.vector.scalar_tensor_tensor(
-                    out=o[:, n, :], in0=t_tiles[i][:, n, :],
-                    scalar=rstd_tiles[i][:, n : n + 1], in1=shift,
+                    out=t[:, m, :], in0=h_tiles[j][:, m, :],
+                    scalar=moment_tiles[i][:, first + m, 1:2], in1=gain,
+                    op0=ALU.subtract, op1=ALU.mult,
+                )
+            t_tiles[j] = t
+
+        def scale_shift_store(j):
+            i, first = tile_of(j, 0)
+            o = work.tile([P, 2, H], F32)
+            for m in range(2):
+                nc.vector.scalar_tensor_tensor(
+                    out=o[:, m, :], in0=t_tiles[j][:, m, :],
+                    scalar=rstd_tiles[i][:, first + m : first + m + 1], in1=shift,
                     op0=ALU.mult, op1=ALU.add,
                 )
-                if n % 2 == 1 or s == 1:
-                    first = max(0, n - 1)
-                    nc.sync.dma_start(out=rows[:, first : n + 1, :], in_=o[:, first : n + 1, :])
+            nc.sync.dma_start(out=rows_of(out, i)[:, first : first + 2, :], in_=o[:])
 
-        def run(stage, i, *args):
-            if 0 <= i < GROUPS:
-                stage(i, *args)
+        def run(stage, j, *args):
+            if 0 <= j < PAIRS:
+                stage(j, *args)
 
         with tc.manual_schedule():
             warm(3)
-            prepare_w()
-            for step in range(-2, GROUPS + 2):
-                run(load_x, step + LOADS_AHEAD)
+            for j in range(2):
+                for m in range(2):
+                    transpose_x(j, m)
+                    copy_xt(j, m)
+            group_w()
+            quantise_x(0)
+            quantise_w()
+            warm(3)
+            for m in range(2):
+                transpose_x(2, m)
+                copy_xt(2, m)
+            column, spread = spread_vectors()
+            nc.vector.tensor_copy(out=bias_col[:], in_=column[:, :, 0])
+            nc.vector.tensor_copy(out=vec[:], in_=spread[:])
+            quantise_x(1)
+            for step in range(PAIRS + 6):
+                if step % 2 == 0 and step // 2 + LOADS_AHEAD < LOADS:
+                    load_x(step // 2 + LOADS_AHEAD)
+                run(multiply, step)
+                run(silu, step)
+                run(transpose_h, step - 1)
+                run(transpose_x, step + 3, 0)
+                run(transpose_x, step + 3, 1)
+                run(centre_and_gain, step - 2)
                 run(moments, step - 1)
-                run(multiply, step, (0,))
-                run(silu, step, (0,))
-                run(quantise_x, step + 1)
-                run(transpose_x, step + 2, 0, 2)
-                run(copy_xt, step + 2, 0, 4)
-                if step == -1:
-                    spread_vectors()
-                run(multiply, step, (1,))
-                run(silu, step, (1,))
-                run(centre_and_gain, step - 1)
                 run(rsqrt, step - 1)
-                run(transpose_x, step + 2, 1, 2)
-                if step == -2:
-                    warm(3)
-                run(copy_xt, step + 2, 1, 4)
-                run(copy_xt, step + 2, 2, 4)
-                run(copy_xt, step + 2, 3, 4)
-                run(transpose_h, step)
-                run(scale_shift_store, step - 2)
+                run(quantise_x, step + 2)
+                run(copy_xt, step + 3, 0)
+                run(copy_xt, step + 3, 1)
+                run(scale_shift_store, step - 4)

@@ -29,7 +29,11 @@ WARM_COLS = 512
 
 
 def on_scalar(j):
-    return j % 3 == 1
+    return j >= 31
+
+
+def shared(j):
+    return j < 28
 
 
 def tile_evidentialhead_pa_t_kernel(tc, x, W1, b1, g, beta, out):
@@ -43,10 +47,12 @@ def tile_evidentialhead_pa_t_kernel(tc, x, W1, b1, g, beta, out):
         stats = stack.enter_context(tc.tile_pool(name="stats", bufs=5))
         xt_psum = stack.enter_context(tc.psum_pool(name="xt_psum", bufs=3))
         z_psum = stack.enter_context(tc.psum_pool(name="z_psum", bufs=2))
-        h_psum = stack.enter_context(tc.psum_pool(name="h_psum", bufs=3))
+        shift_psum = stack.enter_context(tc.psum_pool(name="shift_psum", bufs=1))
+        h_psum = stack.enter_context(tc.psum_pool(name="h_psum", bufs=2))
 
         x_tiles, xt_tiles, grouped_tiles, code_tiles, scale_tiles = {}, {}, {}, {}, {}
         z_tiles, ht_tiles, h_tiles, moment_tiles, rstd_tiles, t_tiles = {}, {}, {}, {}, {}, {}
+        u_tiles = {}
 
         def rows_of(dram, i):
             rows = dram[i * TILES * P : (i + 1) * TILES * P, :]
@@ -115,7 +121,7 @@ def tile_evidentialhead_pa_t_kernel(tc, x, W1, b1, g, beta, out):
                     out=column[:, half, :], lhsT=vec_rows[:, 0, half * P : (half + 1) * P],
                     rhs=ones[:, 0:4], start=True, stop=True,
                 )
-            spread = h_psum.tile([P, 2, H], F32, tag="h")
+            spread = shift_psum.tile([P, 2, H], F32)
             nc.tensor.matmul(
                 out=spread[:], lhsT=ones[:], rhs=vec_rows[:, 1:3, :], start=True, stop=True
             )
@@ -197,7 +203,7 @@ def tile_evidentialhead_pa_t_kernel(tc, x, W1, b1, g, beta, out):
 
         def moments(j):
             i, first = tile_of(j, 0)
-            if first == 0:
+            if i not in moment_tiles:
                 moment_load = stats.tile([P, TILES, 3], F32)
                 moment_tiles[i] = moment_load
             moment = moment_tiles[i][:, first : first + 2, :]
@@ -244,15 +250,26 @@ def tile_evidentialhead_pa_t_kernel(tc, x, W1, b1, g, beta, out):
                 )
             t_tiles[j] = t
 
+        def scale(j):
+            i, first = tile_of(j, 1)
+            u = work.tile([P, H], F32)
+            nc.scalar.activation(
+                out=u[:], in_=t_tiles[j][:, 1, :], func=ACT.Copy,
+                scale=rstd_tiles[i][:, first : first + 1],
+            )
+            u_tiles[j] = u
+
         def scale_shift_store(j):
             i, first = tile_of(j, 0)
             o = work.tile([P, 2, H], F32)
-            for m in range(2):
+            for m in range(1 if shared(j) else 2):
                 nc.vector.scalar_tensor_tensor(
                     out=o[:, m, :], in0=t_tiles[j][:, m, :],
-                    scalar=rstd_tiles[i][:, first + m : first + m + 1], in1=shift,
+                    scalar=rstd_tiles[i][:, first + m : first + m + 1], in1=shift_bank,
                     op0=ALU.mult, op1=ALU.add,
                 )
+            if shared(j):
+                nc.gpsimd.tensor_tensor(out=o[:, 1, :], in0=u_tiles[j][:], in1=shift, op=ALU.add)
             nc.sync.dma_start(out=rows_of(out, i)[:, first : first + 2, :], in_=o[:])
 
         def run(stage, j, *args):
@@ -273,10 +290,11 @@ def tile_evidentialhead_pa_t_kernel(tc, x, W1, b1, g, beta, out):
                 transpose_x(2, m)
                 copy_xt(2, m)
             column, spread = spread_vectors()
+            shift_bank = spread[:, 1, :]
             nc.vector.tensor_copy(out=bias_col[:], in_=column[:, :, 0])
             nc.vector.tensor_copy(out=vec[:], in_=spread[:])
             quantise_x(1)
-            for step in range(PAIRS + 6):
+            for step in range(PAIRS + 4):
                 if step % 2 == 0 and step // 2 + LOADS_AHEAD < LOADS:
                     load_x(step // 2 + LOADS_AHEAD)
                 run(multiply, step)
@@ -290,4 +308,6 @@ def tile_evidentialhead_pa_t_kernel(tc, x, W1, b1, g, beta, out):
                 run(quantise_x, step + 2)
                 run(copy_xt, step + 3, 0)
                 run(copy_xt, step + 3, 1)
+                if shared(step - 4):
+                    run(scale, step - 4)
                 run(scale_shift_store, step - 4)

from contextlib import ExitStack

import concourse.mybir as mybir
from concourse.masks import make_identity

F32 = mybir.dt.float32
BF16 = mybir.dt.bfloat16
U32 = mybir.dt.uint32
U8 = mybir.dt.uint8
FP8X4 = mybir.dt.float8_e4m3fn_x4
ACT = mybir.ActivationFunctionType
ALU = mybir.AluOpType

B, D, H = 8192, 1024, 256
EPS_LN = 1e-5
FLOPS = 2 * B * D * H

P = 128
PASSES = D // (4 * P)
HALVES = H // P
BLOCKS = D // 2 // P
PAIR_ROWS = 2 * P
PAIRS = B // PAIR_ROWS
LOAD_PAIRS = 2
TILES = 2 * LOAD_PAIRS
LOADS = PAIRS // LOAD_PAIRS
LOADS_AHEAD = 5
WARM_COLS = 512


def on_scalar(j):
    return j >= 31


def shared(j):
    return j < 28


def tile_evidentialhead_pa_t_kernel(tc, x, W1, b1, g, beta, out):
    nc = tc.nc
    with ExitStack() as stack:
        const = stack.enter_context(tc.tile_pool(name="const", bufs=1))
        x_pool = stack.enter_context(tc.tile_pool(name="x", bufs=6))
        grouped_pool = stack.enter_context(tc.tile_pool(name="grouped", bufs=5))
        mx_pool = stack.enter_context(tc.tile_pool(name="mx", bufs=4))
        work = stack.enter_context(tc.tile_pool(name="work", bufs=7))
        stats = stack.enter_context(tc.tile_pool(name="stats", bufs=5))
        xt_psum = stack.enter_context(tc.psum_pool(name="xt_psum", bufs=3))
        z_psum = stack.enter_context(tc.psum_pool(name="z_psum", bufs=2))
        shift_psum = stack.enter_context(tc.psum_pool(name="shift_psum", bufs=1))
        h_psum = stack.enter_context(tc.psum_pool(name="h_psum", bufs=2))

        x_tiles, xt_tiles, grouped_tiles, code_tiles, scale_tiles = {}, {}, {}, {}, {}
        z_tiles, ht_tiles, h_tiles, moment_tiles, rstd_tiles, t_tiles = {}, {}, {}, {}, {}, {}
        u_tiles = {}

        def rows_of(dram, i):
            rows = dram[i * TILES * P : (i + 1) * TILES * P, :]
            return rows.rearrange("(p n) k -> p n k", n=TILES)

        def tile_of(j, m):
            return j // LOAD_PAIRS, 2 * (j % LOAD_PAIRS) + m

        def load_x(i, pieces=1):
            x_sb = x_pool.tile([P, TILES, D], BF16)
            count = TILES // pieces
            for n in range(0, TILES, count):
                nc.sync.dma_start(out=x_sb[:, n : n + count, :], in_=rows_of(x, i)[:, n : n + count, :])
            x_tiles[i] = x_sb

        ones = const.tile([P, P], BF16)
        nc.vector.memset(ones[:], 1.0)
        zeros = const.tile([P, WARM_COLS], BF16)
        nc.vector.memset(zeros[:], 0.0)
        table = const.tile([P, 1], F32)
        nc.scalar.activation(out=table[:], in_=ones[:, 0:1], func=ACT.Silu)
        ident = const.tile([P, P], F32)
        make_identity(nc, ident[:])

        load_x(0, pieces=4)
        w_raw = const.tile([P, PASSES, 4, H], BF16)
        nc.sync.dma_start(
            out=w_raw[:].rearrange("p c t h -> p c (t h)"),
            in_=W1.rearrange("(c p t) h -> p c (t h)", c=PASSES, p=P, t=4),
        )
        load_x(1, pieces=2)
        load_x(2)
        vec_rows = const.tile([P, 3, H], BF16)
        nc.vector.memset(vec_rows[:], 0.0)
        nc.scalar.dma_start(out=vec_rows[0:1, 0, :], in_=b1.rearrange("(o h) -> o h", o=1))
        nc.scalar.dma_start(out=vec_rows[0:1, 1, :], in_=g.rearrange("(o h) -> o h", o=1))
        nc.scalar.dma_start(out=vec_rows[0:1, 2, :], in_=beta.rearrange("(o h) -> o h", o=1))
        for i in range(3, LOADS_AHEAD):
            load_x(i)
        neg_half = const.tile([P, TILES], F32)
        nc.vector.memset(neg_half[:], -0.5)

        w_grouped = const.tile([P, PASSES, H, 4], BF16, align_bytes=64)
        w_codes = const.tile([P, PASSES * H], U32, align_bytes=64)
        w_scales = const.tile([P, PASSES * H], U8, align_bytes=64)

        def group_w():
            nc.vector.tensor_copy(out=w_grouped[:], in_=w_raw[:].rearrange("p c t h -> p c h t"))

        def quantise_w():
            nc.vector.quantize_mx(
                out=w_codes[:].bitcast(FP8X4),
                scales=w_scales[:],
                in_=w_grouped[:].rearrange("p c h t -> p (c h t)"),
            )

        bias_col = const.tile([P, HALVES], F32)
        vec = const.tile([P, 2, H], F32)
        gain = vec[:, 0, :]
        shift = vec[:, 1, :]

        def spread_vectors():
            column = h_psum.tile([P, HALVES, 4], F32, tag="h")
            for half in range(HALVES):
                nc.tensor.matmul(
                    out=column[:, half, :], lhsT=vec_rows[:, 0, half * P : (half + 1) * P],
                    rhs=ones[:, 0:4], start=True, stop=True,
                )
            spread = shift_psum.tile([P, 2, H], F32)
            nc.tensor.matmul(
                out=spread[:], lhsT=ones[:], rhs=vec_rows[:, 1:3, :], start=True, stop=True
            )
            return column, spread

        def warm(count):
            for k in range(count):
                idle = h_psum.tile([P, WARM_COLS], F32, tag="h")
                nc.tensor.matmul(out=idle[:], lhsT=ones[:], rhs=zeros[:], start=True, stop=True)

        def transpose_x(j, m):
            i, n = tile_of(j, m)
            x_words = x_tiles[i][:].bitcast(F32)
            xt = xt_psum.tile([P, BLOCKS, P], F32)
            for c in range(PASSES):
                for u in range(2):
                    nc.tensor.transpose(
                        xt[:, 2 * c + u, :],
                        x_words[:, n, 2 * P * c + u : 2 * P * (c + 1) : 2],
                        ident[:],
                    )
            xt_tiles[(j, m)] = xt

        def copy_xt(j, m):
            if j not in grouped_tiles:
                grouped = grouped_pool.tile([P, PASSES * PAIR_ROWS * 4], BF16, align_bytes=64)
                grouped_tiles[j] = grouped
            words = grouped_tiles[j][:].bitcast(F32).rearrange(
                "p (c m r u) -> p c m r u", c=PASSES, m=2, r=P, u=2
            )
            planes = xt_tiles[(j, m)][:].rearrange("p (c u) r -> p c r u", c=PASSES, u=2)
            nc.scalar.copy(out=words[:, :, m, :, :], in_=planes)

        def quantise_x(j):
            codes = mx_pool.tile([P, PASSES * PAIR_ROWS], U32, align_bytes=64)
            scales = mx_pool.tile([P, PASSES * PAIR_ROWS], U8, align_bytes=64)
            nc.vector.quantize_mx(
                out=codes[:].bitcast(FP8X4), scales=scales[:], in_=grouped_tiles[j][:]
            )
            code_tiles[j] = codes
            scale_tiles[j] = scales

        def multiply(j):
            z = z_psum.tile([P, HALVES, PAIR_ROWS], F32)
            for half in range(HALVES):
                for c in range(PASSES):
                    x_cols = slice(c * PAIR_ROWS, (c + 1) * PAIR_ROWS)
                    w_cols = slice(c * H + half * P, c * H + (half + 1) * P)
                    nc.tensor.matmul_mx(
                        out=z[:, half, :],
                        lhsT=w_codes[:, w_cols].bitcast(FP8X4),
                        lhsT_scale=w_scales[:, w_cols],
                        rhs=code_tiles[j][:, x_cols].bitcast(FP8X4),
                        rhs_scale=scale_tiles[j][:, x_cols],
                        start=(c == 0),
                        stop=(c == PASSES - 1),
                    )
            z_tiles[j] = z

        def silu(j):
            ht = work.tile([P, HALVES, PAIR_ROWS], F32)
            for half in range(HALVES):
                nc.scalar.activation(
                    out=ht[:, half, :], in_=z_tiles[j][:, half, :], func=ACT.Silu,
                    bias=bias_col[:, half : half + 1],
                )
            ht_tiles[j] = ht

        def transpose_h(j):
            h = h_psum.tile([P, 2, H], F32, tag="h")
            for m in range(2):
                for half in range(HALVES):
                    nc.tensor.transpose(
                        h[:, m, half * P : (half + 1) * P],
                        ht_tiles[j][:, half, m * P : (m + 1) * P],
                        ident[:],
                    )
            h_tiles[j] = h

        def moments(j):
            i, first = tile_of(j, 0)
            if i not in moment_tiles:
                moment_load = stats.tile([P, TILES, 3], F32)
                moment_tiles[i] = moment_load
            moment = moment_tiles[i][:, first : first + 2, :]
            h = h_tiles[j]
            if on_scalar(j):
                for m in range(2):
                    scratch = work.tile([P, H], F32)
                    nc.scalar.activation(
                        out=scratch[:], in_=h[:, m, :], func=ACT.Copy, scale=1.0 / H,
                        accum_out=moment[:, m, 1:2],
                    )
                for m in range(2):
                    scratch = work.tile([P, H], F32)
                    nc.scalar.activation(
                        out=scratch[:], in_=h[:, m, :], func=ACT.Square, scale=-1.0,
                        bias=moment[:, m, 1:2], accum_out=moment[:, m, 2:3],
                    )
            else:
                nc.vector.bn_stats(
                    out=moment.rearrange("p m s -> p (m s)"), in_=h[:].rearrange("p m h -> p h m")
                )

        def rsqrt(j):
            i, first = tile_of(j, 0)
            if first == 0:
                return
            var_eps = stats.tile([P, TILES], F32)
            nc.gpsimd.tensor_scalar(
                out=var_eps[:], in0=moment_tiles[i][:, :, 2], scalar1=1.0 / H, scalar2=EPS_LN,
                op0=ALU.mult, op1=ALU.add,
            )
            rstd = stats.tile([P, TILES], F32)
            nc.gpsimd.tensor_tensor(out=rstd[:], in0=var_eps[:], in1=neg_half[:], op=ALU.pow)
            rstd_tiles[i] = rstd

        def centre_and_gain(j):
            i, first = tile_of(j, 0)
            t = work.tile([P, 2, H], F32)
            for m in range(2):
                nc.vector.scalar_tensor_tensor(
                    out=t[:, m, :], in0=h_tiles[j][:, m, :],
                    scalar=moment_tiles[i][:, first + m, 1:2], in1=gain,
                    op0=ALU.subtract, op1=ALU.mult,
                )
            t_tiles[j] = t

        def scale(j):
            i, first = tile_of(j, 1)
            u = work.tile([P, H], F32)
            nc.scalar.activation(
                out=u[:], in_=t_tiles[j][:, 1, :], func=ACT.Copy,
                scale=rstd_tiles[i][:, first : first + 1],
            )
            u_tiles[j] = u

        def scale_shift_store(j):
            i, first = tile_of(j, 0)
            o = work.tile([P, 2, H], F32)
            for m in range(1 if shared(j) else 2):
                nc.vector.scalar_tensor_tensor(
                    out=o[:, m, :], in0=t_tiles[j][:, m, :],
                    scalar=rstd_tiles[i][:, first + m : first + m + 1], in1=shift_bank,
                    op0=ALU.mult, op1=ALU.add,
                )
            if shared(j):
                nc.gpsimd.tensor_tensor(out=o[:, 1, :], in0=u_tiles[j][:], in1=shift, op=ALU.add)
            nc.sync.dma_start(out=rows_of(out, i)[:, first : first + 2, :], in_=o[:])

        def run(stage, j, *args):
            if 0 <= j < PAIRS:
                stage(j, *args)

        with tc.manual_schedule():
            warm(3)
            for j in range(2):
                for m in range(2):
                    transpose_x(j, m)
                    copy_xt(j, m)
            group_w()
            quantise_x(0)
            quantise_w()
            warm(3)
            for m in range(2):
                transpose_x(2, m)
                copy_xt(2, m)
            column, spread = spread_vectors()
            shift_bank = spread[:, 1, :]
            nc.vector.tensor_copy(out=bias_col[:], in_=column[:, :, 0])
            nc.vector.tensor_copy(out=vec[:], in_=spread[:])
            quantise_x(1)
            for step in range(PAIRS + 4):
                if step % 2 == 0 and step // 2 + LOADS_AHEAD < LOADS:
                    load_x(step // 2 + LOADS_AHEAD)
                run(multiply, step)
                run(silu, step)
                run(transpose_h, step - 1)
                run(transpose_x, step + 3, 0)
                run(transpose_x, step + 3, 1)
                run(centre_and_gain, step - 2)
                run(moments, step - 1)
                run(rsqrt, step - 1)
                run(quantise_x, step + 2)
                run(copy_xt, step + 3, 0)
                run(copy_xt, step + 3, 1)
                if shared(step - 4):
                    run(scale, step - 4)
                run(scale_shift_store, step - 4)
